import numpy as np
import ml_dtypes


def mxq(x, axis, fmt="e4m3"):
    dtype, down = {"e4m3": (ml_dtypes.float8_e4m3fn, 7), "e5m2": (ml_dtypes.float8_e5m2, 14)}[fmt]
    v = np.moveaxis(np.asarray(x, np.float32).astype(ml_dtypes.bfloat16).astype(np.float64), axis, -1)
    blocks = v.reshape(v.shape[:-1] + (-1, 32))
    amax = np.abs(blocks).max(-1, keepdims=True)
    byte = np.maximum(np.where(amax > 0, np.frexp(amax)[1] - 1 + 127, 0) - down, 1)
    scale = np.exp2(byte - 127.0)
    codes = (blocks / scale).astype(np.float32).astype(dtype).astype(np.float64)
    return np.moveaxis((codes * scale).reshape(v.shape), -1, axis)


WIDE = False


def mx_kscale(k):
    if not WIDE:
        return np.ones(k)
    levels = np.array([10, -10, 5, -5, 0])
    if k % 512:
        return np.exp2(np.random.permutation(np.resize(levels, k // 32))).repeat(32)
    a = np.empty((k // 512, 16))
    for p in range(k // 512):
        a[p, :8] = np.random.permutation(np.resize(levels, 8))
        for g in range(8):
            far = levels[np.abs(levels - a[p, g]) >= 10]
            a[p, g + 8] = far[np.random.randint(len(far))]
    return np.exp2(a.ravel()).repeat(32)


BF16 = ml_dtypes.bfloat16


def bf(x):
    return np.asarray(x, np.float32).astype(BF16)


def f64(x):
    return np.asarray(x).astype(np.float64)


B, NB, NL, NG, NK = 256, 8192, 256, 500, 3
N2 = 2 * NB
L2 = 2 * NL


def relu(v):
    return np.maximum(v, 0.0)


def setup_inputs():
    s, t = mx_kscale(N2), mx_kscale(L2)
    return {'Volt': bf(np.random.standard_normal((B, N2)) * s),
            'IM': bf(np.random.standard_normal((L2, N2)) / np.sqrt(N2) / s[None, :] * t[:, None]),
            'Ybr': bf(np.random.standard_normal((L2, L2)) / np.sqrt(L2) / t[None, :]),
            'L_limit': bf(np.random.random_sample((NL,)) + 0.5),
            'n_o_mu_i_u': bf(np.random.standard_normal((B, NL)))}


def reference(Volt, IM, Ybr, L_limit, n_o_mu_i_u):
    d = mxq(f64(Volt), 1, 'e4m3') @ mxq(f64(IM), 1, 'e4m3').T
    Ibr = mxq(d, 1, 'e4m3') @ mxq(f64(Ybr), 1, 'e4m3').T
    m = Ibr[:, :NL] ** 2 + Ibr[:, NL:] ** 2
    g = m - f64(L_limit) ** 2
    mu = f64(n_o_mu_i_u)
    return relu(g).sum(axis=1) + np.abs(mu * g).sum(axis=1) + relu(-mu).sum(axis=1)

@@ -1,0 +1,283 @@
+from contextlib import ExitStack
+
+import concourse.mybir as mybir
+from concourse.masks import make_identity
+
+F32 = mybir.dt.float32
+BF16 = mybir.dt.bfloat16
+U32 = mybir.dt.uint32
+U8 = mybir.dt.uint8
+FP8X4 = mybir.dt.float8_e4m3fn_x4
+ALU = mybir.AluOpType
+ACT = mybir.ActivationFunctionType
+
+P = 128
+K_PASS = 512
+WORDS = K_PASS // 2
+
+BATCH = 256
+N2 = 16384
+L2 = 512
+NL = L2 // 2
+
+VOLT_TILES = BATCH // P
+IM_TILES = L2 // P
+CHUNK = 4096
+CHUNKS = N2 // CHUNK
+PASSES = CHUNK // K_PASS
+QUANT_COLS = 2048
+
+FLOPS = 2 * BATCH * L2 * N2 + 2 * BATCH * L2 * L2
+
+
+def tile_kktloss_pa_k_kernel(tc, Volt, IM, Ybr, L_limit, n_o_mu_i_u, out):
+    nc = tc.nc
+    with ExitStack() as ctx:
+        keep = ctx.enter_context(tc.tile_pool(name="keep", bufs=1))
+        volt_in = ctx.enter_context(tc.tile_pool(name="volt_in", bufs=2))
+        im_in = ctx.enter_context(tc.tile_pool(name="im_in", bufs=2 * IM_TILES))
+        regroup = ctx.enter_context(tc.tile_pool(name="regroup", bufs=3))
+        volt_mx = ctx.enter_context(tc.tile_pool(name="volt_mx", bufs=2))
+        im_mx = ctx.enter_context(tc.tile_pool(name="im_mx", bufs=3))
+        tail = ctx.enter_context(tc.tile_pool(name="tail", bufs=2))
+        sums = ctx.enter_context(tc.psum_pool(name="sums", bufs=1))
+        banks = ctx.enter_context(tc.psum_pool(name="banks", bufs=4))
+        ctx.enter_context(tc.manual_schedule())
+
+        ident = keep.tile([P, P], F32)
+        make_identity(nc, ident[:])
+        ones = keep.tile([P, P], BF16)
+        nc.vector.memset(ones[:], 1.0)
+        result_cols = keep.tile([P, P], F32)
+        nc.vector.memset(result_cols[:], 0.0)
+
+        def quantise_blocks(blocks, codes, scales):
+            grouped = regroup.tile([P, len(blocks) * K_PASS], BF16, align_bytes=64)
+            grouped_words = grouped[:].bitcast(F32).rearrange(
+                "p (n r u) -> p n r u", r=P, u=2
+            )
+            for pair in range(len(blocks) // 2):
+                bank = banks.tile([P, 2, 2, P], F32, tag="bank")
+                for i in range(2):
+                    for u in range(2):
+                        nc.tensor.transpose(
+                            bank[:, i, u, :],
+                            blocks[2 * pair + i][:, u:WORDS:2],
+                            ident[:],
+                        )
+                copy = nc.vector.tensor_copy if pair % 4 == 2 else nc.scalar.copy
+                copy(
+                    out=grouped_words[:, 2 * pair : 2 * pair + 2],
+                    in_=bank[:].rearrange("p i u r -> p i r u"),
+                )
+            for first in range(0, len(blocks) * K_PASS, QUANT_COLS):
+                packed = slice(first // 4, (first + QUANT_COLS) // 4)
+                nc.vector.quantize_mx(
+                    out=codes[:, packed].bitcast(FP8X4),
+                    scales=scales[:, packed],
+                    in_=grouped[:, first : first + QUANT_COLS],
+                )
+
+        ybr_raw = keep.tile([P, IM_TILES * L2], BF16)
+        nc.sync.dma_start(
+            out=ybr_raw[:].rearrange("p (t j) -> p t j", t=IM_TILES),
+            in_=Ybr.rearrange("(t p) j -> p t j", p=P),
+        )
+        limit_row = keep.tile([P, NL], BF16)
+        nc.vector.memset(limit_row[:], 0.0)
+        nc.sync.dma_start(
+            out=limit_row[0:1, :], in_=L_limit.rearrange("(o l) -> o l", o=1)
+        )
+        mu = keep.tile([P, VOLT_TILES * NL], BF16)
+        nc.sync.dma_start(
+            out=mu[:].rearrange("p (t l) -> p t l", t=VOLT_TILES),
+            in_=n_o_mu_i_u.rearrange("(t p) l -> p t l", p=P),
+        )
+
+        volt_rows = Volt.rearrange("(t p) k -> p t k", p=P)
+        im_rows = IM.rearrange("(p t) k -> t p k", t=IM_TILES)
+
+        def load_chunk(c):
+            cols = slice(c * CHUNK, (c + 1) * CHUNK)
+            volt_raw = volt_in.tile([P, VOLT_TILES * CHUNK], BF16)
+            nc.sync.dma_start(
+                out=volt_raw[:].rearrange("p (t k) -> p t k", t=VOLT_TILES),
+                in_=volt_rows[:, :, cols],
+            )
+            im_raws = []
+            for t in range(IM_TILES):
+                im_raw = im_in.tile([P, CHUNK], BF16)
+                nc.sync.dma_start(out=im_raw[:], in_=im_rows[t, :, cols])
+                im_raws.append(im_raw)
+            return volt_raw, im_raws
+
+        loaded = load_chunk(0)
+
+        ybr_codes = keep.tile([P, L2], U32, align_bytes=64)
+        ybr_scales = keep.tile([P, L2], U8, align_bytes=64)
+        ybr_words = ybr_raw[:].bitcast(F32)
+        quantise_blocks(
+            [ybr_words[:, t * WORDS : (t + 1) * WORDS] for t in range(IM_TILES)],
+            ybr_codes,
+            ybr_scales,
+        )
+
+        limit_all = banks.tile([P, NL], F32, tag="bank")
+        nc.tensor.matmul(
+            out=limit_all[:], lhsT=ones[:], rhs=limit_row[:], start=True, stop=True
+        )
+        limit_sq = keep.tile([P, NL], F32)
+        nc.scalar.activation(out=limit_sq[:], in_=limit_all[:], func=ACT.Square)
+
+        neg_mu_sums = []
+        for bt in range(VOLT_TILES):
+            neg_mu = tail.tile([P, NL], F32)
+            neg_mu_sum = keep.tile([P, 1], F32, name="neg_mu_sum%d" % bt)
+            nc.scalar.activation(
+                out=neg_mu[:],
+                in_=mu[:, bt * NL : (bt + 1) * NL],
+                func=ACT.Relu,
+                scale=-1.0,
+                accum_out=neg_mu_sum[:],
+            )
+            neg_mu_sums.append(neg_mu_sum)
+
+        d_sums = [
+            sums.tile([P, BATCH], F32, name="d_sum%d" % t) for t in range(IM_TILES)
+        ]
+        d_grouped = [
+            keep.tile([P, P, IM_TILES], BF16, name="d_grouped%d" % bt, align_bytes=64)
+            for bt in range(VOLT_TILES)
+        ]
+
+        def multiply(c, t, im_codes, im_scales, volt_codes, volt_scales):
+            for g in range(PASSES):
+                rows = slice(g * P, (g + 1) * P)
+                batch = slice(g * BATCH, (g + 1) * BATCH)
+                nc.tensor.matmul_mx(
+                    out=d_sums[t][:],
+                    lhsT=im_codes[:, rows].bitcast(FP8X4),
+                    lhsT_scale=im_scales[:, rows],
+                    rhs=volt_codes[:, batch].bitcast(FP8X4),
+                    rhs_scale=volt_scales[:, batch],
+                    start=(c == 0 and g == 0),
+                    stop=(c == CHUNKS - 1 and g == PASSES - 1),
+                )
+            if c == CHUNKS - 1:
+                for bt in range(VOLT_TILES):
+                    nc.scalar.copy(
+                        out=d_grouped[bt][:, :, t],
+                        in_=d_sums[t][:, bt * P : (bt + 1) * P],
+                    )
+
+        waiting = None
+        for c in range(CHUNKS):
+            volt_raw, im_raws = loaded
+            if c + 1 < CHUNKS:
+                loaded = load_chunk(c + 1)
+
+            volt_codes = volt_mx.tile([P, PASSES * BATCH], U32, align_bytes=64)
+            volt_scales = volt_mx.tile([P, PASSES * BATCH], U8, align_bytes=64)
+            volt_words = volt_raw[:].bitcast(F32).rearrange(
+                "p (t g w) -> p t g w", t=VOLT_TILES, w=WORDS
+            )
+            step = PASSES // VOLT_TILES
+            for first in range(0, PASSES, step):
+                packed = slice(first * BATCH, (first + step) * BATCH)
+                quantise_blocks(
+                    [
+                        volt_words[:, bt, g, :]
+                        for g in range(first, first + step)
+                        for bt in range(VOLT_TILES)
+                    ],
+                    volt_codes[:, packed],
+                    volt_scales[:, packed],
+                )
+
+            for t in range(IM_TILES):
+                im_codes = im_mx.tile([P, PASSES * P], U32, align_bytes=64)
+                im_scales = im_mx.tile([P, PASSES * P], U8, align_bytes=64)
+                im_words = im_raws[t][:].bitcast(F32)
+                quantise_blocks(
+                    [im_words[:, g * WORDS : (g + 1) * WORDS] for g in range(PASSES)],
+                    im_codes,
+                    im_scales,
+                )
+                if waiting is not None:
+                    multiply(*waiting)
+                waiting = (c, t, im_codes, im_scales, volt_codes, volt_scales)
+        multiply(*waiting)
+
+        currents = []
+        for bt in range(VOLT_TILES):
+            d_codes = keep.tile([P, P], U32, name="d_codes%d" % bt, align_bytes=64)
+            d_scales = keep.tile([P, P], U8, name="d_scales%d" % bt, align_bytes=64)
+            nc.vector.quantize_mx(
+                out=d_codes[:].bitcast(FP8X4),
+                scales=d_scales[:],
+                in_=d_grouped[bt][:].rearrange("p b t -> p (b t)"),
+            )
+            ibr = banks.tile([P, L2], F32, tag="bank")
+            nc.tensor.matmul_mx(
+                out=ibr[:],
+                lhsT=d_codes[:].bitcast(FP8X4),
+                lhsT_scale=d_scales[:],
+                rhs=ybr_codes[:].bitcast(FP8X4),
+                rhs_scale=ybr_scales[:],
+                start=True,
+                stop=True,
+            )
+            currents.append(ibr)
+
+        squares = []
+        for bt in range(VOLT_TILES):
+            square = tail.tile([P, L2], F32)
+            nc.scalar.activation(out=square[:], in_=currents[bt][:], func=ACT.Square)
+            squares.append(square)
+
+        for bt in range(VOLT_TILES):
+            magnitude = tail.tile([P, NL], F32)
+            nc.vector.tensor_tensor(
+                out=magnitude[:], in0=squares[bt][:, :NL], in1=squares[bt][:, NL:], op=ALU.add
+            )
+            excess = tail.tile([P, NL], F32)
+            nc.vector.tensor_tensor(
+                out=excess[:], in0=magnitude[:], in1=limit_sq[:], op=ALU.subtract
+            )
+            over = tail.tile([P, NL], F32)
+            over_sum = tail.tile([P, 1], F32)
+            nc.scalar.activation(
+                out=over[:], in_=excess[:], func=ACT.Relu, accum_out=over_sum[:]
+            )
+            slack = tail.tile([P, NL], F32)
+            nc.vector.tensor_tensor(
+                out=slack[:], in0=excess[:], in1=mu[:, bt * NL : (bt + 1) * NL], op=ALU.mult
+            )
+            slack_abs = tail.tile([P, NL], F32)
+            slack_sum = tail.tile([P, 1], F32)
+            nc.vector.scalar_tensor_tensor(
+                out=slack_abs[:],
+                in0=slack[:],
+                scalar=-1.0,
+                in1=slack[:],
+                op0=ALU.mult,
+                op1=ALU.max,
+                accum_out=slack_sum[:],
+            )
+            nc.vector.tensor_scalar(
+                out=result_cols[:, bt : bt + 1],
+                in0=slack_sum[:],
+                scalar1=over_sum[:],
+                scalar2=neg_mu_sums[bt][:],
+                op0=ALU.add,
+                op1=ALU.add,
+            )
+
+        flipped = banks.tile([P, P], F32, tag="bank")
+        nc.tensor.transpose(flipped[:], result_cols[:], ident[:])
+        result_rows = keep.tile([P, P], F32)
+        nc.vector.tensor_copy(out=result_rows[:], in_=flipped[:])
+        nc.sync.dma_start(
+            out=out.rearrange("(t b) -> t b", t=VOLT_TILES),
+            in_=result_rows[0:VOLT_TILES, :],
+        )

@@ -13,7 +13,8 @@ ACT = mybir.ActivationFunctionType
 
 P = 128
 K_PASS = 512
-WORDS = K_PASS // 2
+RUN = 16
+BLOCK = 2 * RUN
 
 BATCH = 256
 N2 = 16384
@@ -22,10 +23,11 @@ NL = L2 // 2
 
 VOLT_TILES = BATCH // P
 IM_TILES = L2 // P
-CHUNK = 4096
-CHUNKS = N2 // CHUNK
-PASSES = CHUNK // K_PASS
-QUANT_COLS = 2048
+PAIR = 2
+
+CHUNKS = [1024] + 7 * [2048] + [1024]
+LOADS_AHEAD = 8
+YBR_AFTER = 3
 
 FLOPS = 2 * BATCH * L2 * N2 + 2 * BATCH * L2 * L2
 
@@ -34,11 +36,11 @@ def tile_kktloss_pa_k_kernel(tc, Volt, IM, Ybr, L_limit, n_o_mu_i_u, out):
     nc = tc.nc
     with ExitStack() as ctx:
         keep = ctx.enter_context(tc.tile_pool(name="keep", bufs=1))
-        volt_in = ctx.enter_context(tc.tile_pool(name="volt_in", bufs=2))
-        im_in = ctx.enter_context(tc.tile_pool(name="im_in", bufs=2 * IM_TILES))
+        raw_in = ctx.enter_context(tc.tile_pool(name="raw_in", bufs=LOADS_AHEAD))
+        sorted_in = ctx.enter_context(tc.tile_pool(name="sorted_in", bufs=3))
         regroup = ctx.enter_context(tc.tile_pool(name="regroup", bufs=3))
-        volt_mx = ctx.enter_context(tc.tile_pool(name="volt_mx", bufs=2))
-        im_mx = ctx.enter_context(tc.tile_pool(name="im_mx", bufs=3))
+        volt_mx = ctx.enter_context(tc.tile_pool(name="volt_mx", bufs=3))
+        im_mx = ctx.enter_context(tc.tile_pool(name="im_mx", bufs=4))
         tail = ctx.enter_context(tc.tile_pool(name="tail", bufs=2))
         sums = ctx.enter_context(tc.psum_pool(name="sums", bufs=1))
         banks = ctx.enter_context(tc.psum_pool(name="banks", bufs=4))
@@ -51,162 +53,191 @@ def tile_kktloss_pa_k_kernel(tc, Volt, IM, Ybr, L_limit, n_o_mu_i_u, out):
         result_cols = keep.tile([P, P], F32)
         nc.vector.memset(result_cols[:], 0.0)
 
-        def quantise_blocks(blocks, codes, scales):
-            grouped = regroup.tile([P, len(blocks) * K_PASS], BF16, align_bytes=64)
-            grouped_words = grouped[:].bitcast(F32).rearrange(
-                "p (n r u) -> p n r u", r=P, u=2
-            )
-            for pair in range(len(blocks) // 2):
-                bank = banks.tile([P, 2, 2, P], F32, tag="bank")
-                for i in range(2):
-                    for u in range(2):
-                        nc.tensor.transpose(
-                            bank[:, i, u, :],
-                            blocks[2 * pair + i][:, u:WORDS:2],
-                            ident[:],
-                        )
-                copy = nc.vector.tensor_copy if pair % 4 == 2 else nc.scalar.copy
-                copy(
-                    out=grouped_words[:, 2 * pair : 2 * pair + 2],
-                    in_=bank[:].rearrange("p i u r -> p i r u"),
-                )
-            for first in range(0, len(blocks) * K_PASS, QUANT_COLS):
-                packed = slice(first // 4, (first + QUANT_COLS) // 4)
-                nc.vector.quantize_mx(
-                    out=codes[:, packed].bitcast(FP8X4),
-                    scales=scales[:, packed],
-                    in_=grouped[:, first : first + QUANT_COLS],
-                )
-
-        ybr_raw = keep.tile([P, IM_TILES * L2], BF16)
-        nc.sync.dma_start(
-            out=ybr_raw[:].rearrange("p (t j) -> p t j", t=IM_TILES),
-            in_=Ybr.rearrange("(t p) j -> p t j", p=P),
-        )
-        limit_row = keep.tile([P, NL], BF16)
-        nc.vector.memset(limit_row[:], 0.0)
-        nc.sync.dma_start(
-            out=limit_row[0:1, :], in_=L_limit.rearrange("(o l) -> o l", o=1)
-        )
-        mu = keep.tile([P, VOLT_TILES * NL], BF16)
-        nc.sync.dma_start(
-            out=mu[:].rearrange("p (t l) -> p t l", t=VOLT_TILES),
-            in_=n_o_mu_i_u.rearrange("(t p) l -> p t l", p=P),
-        )
-
-        volt_rows = Volt.rearrange("(t p) k -> p t k", p=P)
-        im_rows = IM.rearrange("(p t) k -> t p k", t=IM_TILES)
-
-        def load_chunk(c):
-            cols = slice(c * CHUNK, (c + 1) * CHUNK)
-            volt_raw = volt_in.tile([P, VOLT_TILES * CHUNK], BF16)
-            nc.sync.dma_start(
-                out=volt_raw[:].rearrange("p (t k) -> p t k", t=VOLT_TILES),
-                in_=volt_rows[:, :, cols],
-            )
-            im_raws = []
-            for t in range(IM_TILES):
-                im_raw = im_in.tile([P, CHUNK], BF16)
-                nc.sync.dma_start(out=im_raw[:], in_=im_rows[t, :, cols])
-                im_raws.append(im_raw)
-            return volt_raw, im_raws
-
-        loaded = load_chunk(0)
-
-        ybr_codes = keep.tile([P, L2], U32, align_bytes=64)
-        ybr_scales = keep.tile([P, L2], U8, align_bytes=64)
-        ybr_words = ybr_raw[:].bitcast(F32)
-        quantise_blocks(
-            [ybr_words[:, t * WORDS : (t + 1) * WORDS] for t in range(IM_TILES)],
-            ybr_codes,
-            ybr_scales,
-        )
-
-        limit_all = banks.tile([P, NL], F32, tag="bank")
-        nc.tensor.matmul(
-            out=limit_all[:], lhsT=ones[:], rhs=limit_row[:], start=True, stop=True
-        )
-        limit_sq = keep.tile([P, NL], F32)
-        nc.scalar.activation(out=limit_sq[:], in_=limit_all[:], func=ACT.Square)
-
-        neg_mu_sums = []
-        for bt in range(VOLT_TILES):
-            neg_mu = tail.tile([P, NL], F32)
-            neg_mu_sum = keep.tile([P, 1], F32, name="neg_mu_sum%d" % bt)
-            nc.scalar.activation(
-                out=neg_mu[:],
-                in_=mu[:, bt * NL : (bt + 1) * NL],
-                func=ACT.Relu,
-                scale=-1.0,
-                accum_out=neg_mu_sum[:],
-            )
-            neg_mu_sums.append(neg_mu_sum)
-
         d_sums = [
             sums.tile([P, BATCH], F32, name="d_sum%d" % t) for t in range(IM_TILES)
         ]
+
+        volt_rows = Volt.rearrange("(t p) k -> p t k", p=P)
+        im_rows = IM.rearrange("(p t) k -> p t k", t=IM_TILES)
+
+        def transpose_out(halves, grouped):
+            words = grouped.bitcast(F32).rearrange("p (n r u) -> p n r u", r=P, u=2)
+            for first in range(0, len(halves), 2):
+                bank = banks.tile([P, 2, 2, P], F32, tag="bank")
+                for i in range(2):
+                    for u in range(2):
+                        nc.tensor.transpose(bank[:, i, u, :], halves[first + i][u], ident[:])
+                nc.scalar.copy(
+                    out=words[:, first : first + 2],
+                    in_=bank[:].rearrange("p i u r -> p i r u"),
+                )
+
+        def quantise(grouped, codes, scales):
+            nc.vector.quantize_mx(out=codes[:].bitcast(FP8X4), scales=scales[:], in_=grouped[:])
+
+        def load(stage):
+            width, rows, cols = stage["width"], stage["rows"], stage["cols"]
+            raw = raw_in.tile([P, PAIR * width], BF16, align_bytes=64)
+            nc.sync.dma_start(
+                out=raw[:].rearrange("p (r k) -> p r k", r=PAIR), in_=rows[:, :, cols]
+            )
+            stage["raw"] = raw
+
+        def sort(stage):
+            in_order = sorted_in.tile([P, PAIR * stage["width"]], BF16, align_bytes=64)
+            nc.vector.tensor_copy(
+                out=in_order[:].rearrange("p (u n x) -> p u n x", u=2, x=RUN),
+                in_=stage["raw"][:].rearrange("p (n u x) -> p u n x", u=2, x=RUN),
+            )
+            stage["sorted"] = in_order
+
+        def transpose(stage):
+            width = stage["width"]
+            words = stage["sorted"][:].bitcast(F32).rearrange(
+                "p (u r w) -> p u r w", u=2, r=PAIR
+            )
+            grouped = regroup.tile([P, PAIR * width], BF16, align_bytes=64)
+            transpose_out(
+                [
+                    [words[:, u, r, g * P : (g + 1) * P] for u in range(2)]
+                    for g in range(width // K_PASS)
+                    for r in range(PAIR)
+                ],
+                grouped[:],
+            )
+            stage["grouped"] = grouped
+
+        def quantise_stage(stage):
+            columns = PAIR * stage["width"] // 4
+            pool = volt_mx if stage["im_tiles"] is None else im_mx
+            codes = pool.tile([P, columns], U32, name="codes", align_bytes=64)
+            scales = pool.tile([P, columns], U8, name="scales", align_bytes=64)
+            quantise(stage["grouped"], codes, scales)
+            stage["mx"] = (codes, scales)
+
+        def multiply(stage):
+            if stage["im_tiles"] is None:
+                return
+            im_codes, im_scales = stage["mx"]
+            volt_codes, volt_scales = stage["volt"]["mx"]
+            passes = stage["width"] // K_PASS
+            for r, t in enumerate(stage["im_tiles"]):
+                for g in range(passes):
+                    rows = slice((PAIR * g + r) * P, (PAIR * g + r + 1) * P)
+                    batch = slice(g * BATCH, (g + 1) * BATCH)
+                    nc.tensor.matmul_mx(
+                        out=d_sums[t][:],
+                        lhsT=im_codes[:, rows].bitcast(FP8X4),
+                        lhsT_scale=im_scales[:, rows],
+                        rhs=volt_codes[:, batch].bitcast(FP8X4),
+                        rhs_scale=volt_scales[:, batch],
+                        start=(stage["first"] and g == 0),
+                        stop=(stage["last"] and g == passes - 1),
+                    )
+
+        stages = []
+        start_col = 0
+        for c, width in enumerate(CHUNKS):
+            cols = slice(start_col, start_col + width)
+            start_col += width
+            common = {
+                "width": width,
+                "cols": cols,
+                "first": c == 0,
+                "last": c == len(CHUNKS) - 1,
+            }
+            volt = dict(common, rows=volt_rows, im_tiles=None)
+            stages.append(volt)
+            for t in range(0, IM_TILES, PAIR):
+                stages.append(
+                    dict(
+                        common,
+                        rows=im_rows[:, t : t + PAIR, :],
+                        im_tiles=range(t, t + PAIR),
+                        volt=volt,
+                    )
+                )
+            if c == YBR_AFTER:
+                ybr_stage = len(stages)
+
+        ybr_raw = keep.tile([P, IM_TILES * L2], BF16)
+        limit_row = keep.tile([P, NL], BF16)
+        nc.vector.memset(limit_row[:], 0.0)
+        mu = keep.tile([P, VOLT_TILES * NL], BF16)
+        ybr_grouped = keep.tile([P, IM_TILES * L2], BF16, align_bytes=64)
+        ybr_codes = keep.tile([P, L2], U32, align_bytes=64)
+        ybr_scales = keep.tile([P, L2], U8, align_bytes=64)
+        limit_sq = keep.tile([P, NL], F32)
+        neg_mu_sums = [
+            keep.tile([P, 1], F32, name="neg_mu_sum%d" % bt) for bt in range(VOLT_TILES)
+        ]
+
+        def load_small():
+            nc.sync.dma_start(
+                out=ybr_raw[:].rearrange("p (t j) -> p t j", t=IM_TILES),
+                in_=Ybr.rearrange("(t p) j -> p t j", p=P),
+            )
+            nc.sync.dma_start(
+                out=mu[:].rearrange("p (t l) -> p t l", t=VOLT_TILES),
+                in_=n_o_mu_i_u.rearrange("(t p) l -> p t l", p=P),
+            )
+            nc.sync.dma_start(
+                out=limit_row[0:1, :], in_=L_limit.rearrange("(o l) -> o l", o=1)
+            )
+
+        def prepare_small():
+            words = ybr_raw[:].bitcast(F32).rearrange("p (t w) -> p t w", t=IM_TILES)
+            transpose_out(
+                [[words[:, t, u : L2 // 2 : 2] for u in range(2)] for t in range(IM_TILES)],
+                ybr_grouped[:],
+            )
+            limit_all = banks.tile([P, NL], F32, tag="bank")
+            nc.tensor.matmul(
+                out=limit_all[:], lhsT=ones[:], rhs=limit_row[:], start=True, stop=True
+            )
+            nc.scalar.activation(out=limit_sq[:], in_=limit_all[:], func=ACT.Square)
+            for bt in range(VOLT_TILES):
+                neg_mu = tail.tile([P, NL], F32)
+                nc.scalar.activation(
+                    out=neg_mu[:],
+                    in_=mu[:, bt * NL : (bt + 1) * NL],
+                    func=ACT.Relu,
+                    scale=-1.0,
+                    accum_out=neg_mu_sums[bt][:],
+                )
+
+        n = len(stages)
+
+        def load_stage(s):
+            if s == ybr_stage:
+                load_small()
+            if s < n:
+                load(stages[s])
+
+        for s in range(LOADS_AHEAD):
+            load_stage(s)
+        for i in range(-1, n + 2):
+            if i + 1 < n:
+                sort(stages[i + 1])
+                load_stage(i + 1 + LOADS_AHEAD)
+            if 0 <= i < n:
+                transpose(stages[i])
+            if i == ybr_stage:
+                prepare_small()
+            if 0 <= i - 1 < n:
+                quantise_stage(stages[i - 1])
+            if i == ybr_stage + 1:
+                quantise(ybr_grouped, ybr_codes, ybr_scales)
+            if 0 <= i - 2:
+                multiply(stages[i - 2])
+
         d_grouped = [
             keep.tile([P, P, IM_TILES], BF16, name="d_grouped%d" % bt, align_bytes=64)
             for bt in range(VOLT_TILES)
         ]
-
-        def multiply(c, t, im_codes, im_scales, volt_codes, volt_scales):
-            for g in range(PASSES):
-                rows = slice(g * P, (g + 1) * P)
-                batch = slice(g * BATCH, (g + 1) * BATCH)
-                nc.tensor.matmul_mx(
-                    out=d_sums[t][:],
-                    lhsT=im_codes[:, rows].bitcast(FP8X4),
-                    lhsT_scale=im_scales[:, rows],
-                    rhs=volt_codes[:, batch].bitcast(FP8X4),
-                    rhs_scale=volt_scales[:, batch],
-                    start=(c == 0 and g == 0),
-                    stop=(c == CHUNKS - 1 and g == PASSES - 1),
-                )
-            if c == CHUNKS - 1:
-                for bt in range(VOLT_TILES):
-                    nc.scalar.copy(
-                        out=d_grouped[bt][:, :, t],
-                        in_=d_sums[t][:, bt * P : (bt + 1) * P],
-                    )
-
-        waiting = None
-        for c in range(CHUNKS):
-            volt_raw, im_raws = loaded
-            if c + 1 < CHUNKS:
-                loaded = load_chunk(c + 1)
-
-            volt_codes = volt_mx.tile([P, PASSES * BATCH], U32, align_bytes=64)
-            volt_scales = volt_mx.tile([P, PASSES * BATCH], U8, align_bytes=64)
-            volt_words = volt_raw[:].bitcast(F32).rearrange(
-                "p (t g w) -> p t g w", t=VOLT_TILES, w=WORDS
-            )
-            step = PASSES // VOLT_TILES
-            for first in range(0, PASSES, step):
-                packed = slice(first * BATCH, (first + step) * BATCH)
-                quantise_blocks(
-                    [
-                        volt_words[:, bt, g, :]
-                        for g in range(first, first + step)
-                        for bt in range(VOLT_TILES)
-                    ],
-                    volt_codes[:, packed],
-                    volt_scales[:, packed],
-                )
-
-            for t in range(IM_TILES):
-                im_codes = im_mx.tile([P, PASSES * P], U32, align_bytes=64)
-                im_scales = im_mx.tile([P, PASSES * P], U8, align_bytes=64)
-                im_words = im_raws[t][:].bitcast(F32)
-                quantise_blocks(
-                    [im_words[:, g * WORDS : (g + 1) * WORDS] for g in range(PASSES)],
-                    im_codes,
-                    im_scales,
-                )
-                if waiting is not None:
-                    multiply(*waiting)
-                waiting = (c, t, im_codes, im_scales, volt_codes, volt_scales)
-        multiply(*waiting)
+        for t in range(IM_TILES):
+            for bt, copy in enumerate((nc.scalar.copy, nc.vector.tensor_copy)):
+                copy(out=d_grouped[bt][:, :, t], in_=d_sums[t][:, bt * P : (bt + 1) * P])
 
         currents = []
         for bt in range(VOLT_TILES):

@@ -61,15 +61,17 @@ def tile_kktloss_pa_k_kernel(tc, Volt, IM, Ybr, L_limit, n_o_mu_i_u, out):
         im_rows = IM.rearrange("(p t) k -> p t k", t=IM_TILES)
 
         def transpose_out(halves, grouped):
-            words = grouped.bitcast(F32).rearrange("p (n r u) -> p n r u", r=P, u=2)
+            words = grouped.bitcast(F32).rearrange("p (b c w u) -> p b c u w", c=P, w=2, u=2)
             for first in range(0, len(halves), 2):
-                bank = banks.tile([P, 2, 2, P], F32, tag="bank")
+                bank = banks.tile([P, 2, 2 * P], F32, tag="bank")
                 for i in range(2):
                     for u in range(2):
-                        nc.tensor.transpose(bank[:, i, u, :], halves[first + i][u], ident[:])
+                        nc.tensor.transpose(
+                            bank[:, u, i * P : (i + 1) * P], halves[first + i][u], ident[:]
+                        )
                 nc.scalar.copy(
-                    out=words[:, first : first + 2],
-                    in_=bank[:].rearrange("p i u r -> p i r u"),
+                    out=words[:, first // 2],
+                    in_=bank[:].rearrange("p u (c w) -> p c u w", w=2),
                 )
 
         def quantise(grouped, codes, scales):

@@ -14,7 +14,6 @@ ACT = mybir.ActivationFunctionType
 P = 128
 K_PASS = 512
 RUN = 16
-BLOCK = 2 * RUN
 
 BATCH = 256
 N2 = 16384
@@ -23,11 +22,15 @@ NL = L2 // 2
 
 VOLT_TILES = BATCH // P
 IM_TILES = L2 // P
+ROW_TILES = VOLT_TILES + IM_TILES
 PAIR = 2
 
-CHUNKS = [1024] + 7 * [2048] + [1024]
-LOADS_AHEAD = 8
-YBR_AFTER = 3
+CHUNKS = [512, 512] + 3 * [1024] + 5 * [2048] + [1024, 512, 512]
+CHUNK_BUFFERS = 3
+VOLT_PASSES = 2
+YBR_CHUNK = 5
+QUANTISE_LAG = 2
+MULTIPLY_LAG = 4
 
 FLOPS = 2 * BATCH * L2 * N2 + 2 * BATCH * L2 * L2
 
@@ -36,14 +39,13 @@ def tile_kktloss_pa_k_kernel(tc, Volt, IM, Ybr, L_limit, n_o_mu_i_u, out):
     nc = tc.nc
     with ExitStack() as ctx:
         keep = ctx.enter_context(tc.tile_pool(name="keep", bufs=1))
-        raw_in = ctx.enter_context(tc.tile_pool(name="raw_in", bufs=LOADS_AHEAD))
-        sorted_in = ctx.enter_context(tc.tile_pool(name="sorted_in", bufs=3))
-        regroup = ctx.enter_context(tc.tile_pool(name="regroup", bufs=3))
-        volt_mx = ctx.enter_context(tc.tile_pool(name="volt_mx", bufs=3))
-        im_mx = ctx.enter_context(tc.tile_pool(name="im_mx", bufs=4))
+        raw_in = ctx.enter_context(tc.tile_pool(name="raw_in", bufs=CHUNK_BUFFERS))
+        sorted_in = ctx.enter_context(tc.tile_pool(name="sorted_in", bufs=2))
+        regroup = ctx.enter_context(tc.tile_pool(name="regroup", bufs=4))
+        mx = ctx.enter_context(tc.tile_pool(name="mx", bufs=6))
         tail = ctx.enter_context(tc.tile_pool(name="tail", bufs=2))
         sums = ctx.enter_context(tc.psum_pool(name="sums", bufs=1))
-        banks = ctx.enter_context(tc.psum_pool(name="banks", bufs=4))
+        banks = ctx.enter_context(tc.psum_pool(name="banks", bufs=6))
         ctx.enter_context(tc.manual_schedule())
 
         ident = keep.tile([P, P], F32)
@@ -52,15 +54,17 @@ def tile_kktloss_pa_k_kernel(tc, Volt, IM, Ybr, L_limit, n_o_mu_i_u, out):
         nc.vector.memset(ones[:], 1.0)
         result_cols = keep.tile([P, P], F32)
         nc.vector.memset(result_cols[:], 0.0)
+        limit_row = keep.tile([P, NL], BF16)
+        nc.vector.memset(limit_row[:], 0.0)
 
         d_sums = [
-            sums.tile([P, BATCH], F32, name="d_sum%d" % t) for t in range(IM_TILES)
+            sums.tile([P, L2], F32, name="d_sum%d" % bt) for bt in range(VOLT_TILES)
         ]
 
         volt_rows = Volt.rearrange("(t p) k -> p t k", p=P)
-        im_rows = IM.rearrange("(p t) k -> p t k", t=IM_TILES)
+        im_rows = IM.rearrange("(t p) k -> p t k", p=P)
 
-        def transpose_out(halves, grouped):
+        def transpose(halves, grouped, copies):
             words = grouped.bitcast(F32).rearrange("p (b c w u) -> p b c u w", c=P, w=2, u=2)
             for first in range(0, len(halves), 2):
                 bank = banks.tile([P, 2, 2 * P], F32, tag="bank")
@@ -69,107 +73,119 @@ def tile_kktloss_pa_k_kernel(tc, Volt, IM, Ybr, L_limit, n_o_mu_i_u, out):
                         nc.tensor.transpose(
                             bank[:, u, i * P : (i + 1) * P], halves[first + i][u], ident[:]
                         )
-                nc.scalar.copy(
+                copies[first // 2 % len(copies)](
                     out=words[:, first // 2],
                     in_=bank[:].rearrange("p u (c w) -> p c u w", w=2),
                 )
 
-        def quantise(grouped, codes, scales):
-            nc.vector.quantize_mx(out=codes[:].bitcast(FP8X4), scales=scales[:], in_=grouped[:])
+        def load(chunk):
+            width, cols = chunk["width"], chunk["cols"]
+            chunk["raw"] = []
+            for name, rows in (
+                ("volt_raw", volt_rows),
+                ("im_raw0", im_rows[:, :PAIR, :]),
+                ("im_raw1", im_rows[:, PAIR:, :]),
+            ):
+                raw = raw_in.tile([P, PAIR * width], BF16, name=name, align_bytes=64)
+                nc.sync.dma_start(
+                    out=raw[:].rearrange("p (t k) -> p t k", t=PAIR), in_=rows[:, :, cols]
+                )
+                chunk["raw"].append(raw)
 
-        def load(stage):
-            width, rows, cols = stage["width"], stage["rows"], stage["cols"]
-            raw = raw_in.tile([P, PAIR * width], BF16, align_bytes=64)
-            nc.sync.dma_start(
-                out=raw[:].rearrange("p (r k) -> p r k", r=PAIR), in_=rows[:, :, cols]
+        def sort(chunk, pair):
+            in_order = sorted_in.tile(
+                [P, PAIR * chunk["width"]], BF16, name="in_order%d" % pair, align_bytes=64
             )
-            stage["raw"] = raw
-
-        def sort(stage):
-            in_order = sorted_in.tile([P, PAIR * stage["width"]], BF16, align_bytes=64)
             nc.vector.tensor_copy(
                 out=in_order[:].rearrange("p (u n x) -> p u n x", u=2, x=RUN),
-                in_=stage["raw"][:].rearrange("p (n u x) -> p u n x", u=2, x=RUN),
+                in_=chunk["raw"][pair][:].rearrange("p (n u x) -> p u n x", u=2, x=RUN),
             )
-            stage["sorted"] = in_order
+            words = in_order[:].bitcast(F32).rearrange("p (u r w) -> p u r w", u=2, r=PAIR)
+            chunk["words"] += [words[:, :, r] for r in range(PAIR)]
 
-        def transpose(stage):
-            width = stage["width"]
-            words = stage["sorted"][:].bitcast(F32).rearrange(
-                "p (u r w) -> p u r w", u=2, r=PAIR
+        def blocks(chunk, g, tiles):
+            cols = slice(g * P, (g + 1) * P)
+            return [[chunk["words"][t][:, u, cols] for u in range(2)] for t in tiles]
+
+        def quantise(operand):
+            columns = operand["columns"]
+            codes = mx.tile([P, columns], U32, name=operand["name"] + "_codes", align_bytes=64)
+            scales = mx.tile([P, columns], U8, name=operand["name"] + "_scales", align_bytes=64)
+            nc.vector.quantize_mx(
+                out=codes[:].bitcast(FP8X4), scales=scales[:], in_=operand["grouped"][:]
             )
-            grouped = regroup.tile([P, PAIR * width], BF16, align_bytes=64)
-            transpose_out(
-                [
-                    [words[:, u, r, g * P : (g + 1) * P] for u in range(2)]
-                    for g in range(width // K_PASS)
-                    for r in range(PAIR)
-                ],
-                grouped[:],
-            )
-            stage["grouped"] = grouped
+            operand["mx"] = (codes, scales)
 
-        def quantise_stage(stage):
-            columns = PAIR * stage["width"] // 4
-            pool = volt_mx if stage["im_tiles"] is None else im_mx
-            codes = pool.tile([P, columns], U32, name="codes", align_bytes=64)
-            scales = pool.tile([P, columns], U8, name="scales", align_bytes=64)
-            quantise(stage["grouped"], codes, scales)
-            stage["mx"] = (codes, scales)
-
-        def multiply(stage):
-            if stage["im_tiles"] is None:
-                return
-            im_codes, im_scales = stage["mx"]
-            volt_codes, volt_scales = stage["volt"]["mx"]
-            passes = stage["width"] // K_PASS
-            for r, t in enumerate(stage["im_tiles"]):
-                for g in range(passes):
-                    rows = slice((PAIR * g + r) * P, (PAIR * g + r + 1) * P)
-                    batch = slice(g * BATCH, (g + 1) * BATCH)
-                    nc.tensor.matmul_mx(
-                        out=d_sums[t][:],
-                        lhsT=im_codes[:, rows].bitcast(FP8X4),
-                        lhsT_scale=im_scales[:, rows],
-                        rhs=volt_codes[:, batch].bitcast(FP8X4),
-                        rhs_scale=volt_scales[:, batch],
-                        start=(stage["first"] and g == 0),
-                        stop=(stage["last"] and g == passes - 1),
-                    )
-
-        stages = []
-        start_col = 0
-        for c, width in enumerate(CHUNKS):
-            cols = slice(start_col, start_col + width)
-            start_col += width
-            common = {
-                "width": width,
-                "cols": cols,
-                "first": c == 0,
-                "last": c == len(CHUNKS) - 1,
-            }
-            volt = dict(common, rows=volt_rows, im_tiles=None)
-            stages.append(volt)
-            for t in range(0, IM_TILES, PAIR):
-                stages.append(
-                    dict(
-                        common,
-                        rows=im_rows[:, t : t + PAIR, :],
-                        im_tiles=range(t, t + PAIR),
-                        volt=volt,
-                    )
+        def transpose_pass(item):
+            chunk, g = item["chunk"], item["pass"]
+            volt = item["volt"]
+            if "grouped" not in volt:
+                volt["grouped"] = regroup.tile(
+                    [P, 4 * volt["columns"]], BF16, name="volt_grouped", align_bytes=64
                 )
-            if c == YBR_AFTER:
-                ybr_stage = len(stages)
+            first = item["volt_column"] * 4
+            transpose(
+                blocks(chunk, g, range(VOLT_TILES)),
+                volt["grouped"][:, first : first + 4 * BATCH],
+                [nc.scalar.copy],
+            )
+            grouped = regroup.tile([P, 4 * L2], BF16, name="im_grouped", align_bytes=64)
+            transpose(
+                blocks(chunk, g, range(VOLT_TILES, ROW_TILES)), grouped[:], [nc.scalar.copy]
+            )
+            item["im"] = {"name": "im", "columns": L2, "grouped": grouped}
+
+        def quantise_pass(item):
+            if item["closes_volt"]:
+                quantise(item["volt"])
+            quantise(item["im"])
+
+        def multiply(item):
+            (volt_codes, volt_scales), (im_codes, im_scales) = item["volt"]["mx"], item["im"]["mx"]
+            for bt in range(VOLT_TILES):
+                first = item["volt_column"] + bt * P
+                nc.tensor.matmul_mx(
+                    out=d_sums[bt][:],
+                    lhsT=volt_codes[:, first : first + P].bitcast(FP8X4),
+                    lhsT_scale=volt_scales[:, first : first + P],
+                    rhs=im_codes[:].bitcast(FP8X4),
+                    rhs_scale=im_scales[:],
+                    start=item["first"],
+                    stop=item["last"],
+                )
+
+        chunks = []
+        items = []
+        start_col = 0
+        for width in CHUNKS:
+            chunk = {"width": width, "cols": slice(start_col, start_col + width), "words": []}
+            start_col += width
+            chunk["items"] = []
+            for g in range(width // K_PASS):
+                if g % VOLT_PASSES == 0:
+                    together = min(VOLT_PASSES, width // K_PASS - g)
+                    volt = {"name": "volt", "columns": together * BATCH}
+                item = {
+                    "chunk": chunk,
+                    "pass": g,
+                    "volt": volt,
+                    "volt_column": g % VOLT_PASSES * BATCH,
+                    "closes_volt": g % VOLT_PASSES == together - 1,
+                    "first": len(items) == 0,
+                    "last": len(items) == N2 // K_PASS - 1,
+                }
+                chunk["items"].append(item)
+                items.append(item)
+            chunks.append(chunk)
 
         ybr_raw = keep.tile([P, IM_TILES * L2], BF16)
-        limit_row = keep.tile([P, NL], BF16)
-        nc.vector.memset(limit_row[:], 0.0)
         mu = keep.tile([P, VOLT_TILES * NL], BF16)
         ybr_grouped = keep.tile([P, IM_TILES * L2], BF16, align_bytes=64)
         ybr_codes = keep.tile([P, L2], U32, align_bytes=64)
         ybr_scales = keep.tile([P, L2], U8, align_bytes=64)
         limit_sq = keep.tile([P, NL], F32)
+        mu_abs = keep.tile([P, VOLT_TILES * NL], F32)
+        neg_mu = keep.tile([P, NL], F32)
         neg_mu_sums = [
             keep.tile([P, 1], F32, name="neg_mu_sum%d" % bt) for bt in range(VOLT_TILES)
         ]
@@ -189,17 +205,18 @@ def tile_kktloss_pa_k_kernel(tc, Volt, IM, Ybr, L_limit, n_o_mu_i_u, out):
 
         def prepare_small():
             words = ybr_raw[:].bitcast(F32).rearrange("p (t w) -> p t w", t=IM_TILES)
-            transpose_out(
+            transpose(
                 [[words[:, t, u : L2 // 2 : 2] for u in range(2)] for t in range(IM_TILES)],
                 ybr_grouped[:],
+                [nc.scalar.copy],
             )
             limit_all = banks.tile([P, NL], F32, tag="bank")
             nc.tensor.matmul(
                 out=limit_all[:], lhsT=ones[:], rhs=limit_row[:], start=True, stop=True
             )
             nc.scalar.activation(out=limit_sq[:], in_=limit_all[:], func=ACT.Square)
+            nc.scalar.activation(out=mu_abs[:], in_=mu[:], func=ACT.Abs)
             for bt in range(VOLT_TILES):
-                neg_mu = tail.tile([P, NL], F32)
                 nc.scalar.activation(
                     out=neg_mu[:],
                     in_=mu[:, bt * NL : (bt + 1) * NL],
@@ -208,47 +225,69 @@ def tile_kktloss_pa_k_kernel(tc, Volt, IM, Ybr, L_limit, n_o_mu_i_u, out):
                     accum_out=neg_mu_sums[bt][:],
                 )
 
-        n = len(stages)
+        def quantise_ybr():
+            nc.vector.quantize_mx(
+                out=ybr_codes[:].bitcast(FP8X4), scales=ybr_scales[:], in_=ybr_grouped[:]
+            )
 
-        def load_stage(s):
-            if s == ybr_stage:
+        def load_chunk(c):
+            if c < len(chunks):
+                load(chunks[c])
+            if c == YBR_CHUNK - 1:
                 load_small()
-            if s < n:
-                load(stages[s])
 
-        for s in range(LOADS_AHEAD):
-            load_stage(s)
-        for i in range(-1, n + 2):
-            if i + 1 < n:
-                sort(stages[i + 1])
-                load_stage(i + 1 + LOADS_AHEAD)
-            if 0 <= i < n:
-                transpose(stages[i])
-            if i == ybr_stage:
-                prepare_small()
-            if 0 <= i - 1 < n:
-                quantise_stage(stages[i - 1])
-            if i == ybr_stage + 1:
-                quantise(ybr_grouped, ybr_codes, ybr_scales)
-            if 0 <= i - 2:
-                multiply(stages[i - 2])
+        for c in range(CHUNK_BUFFERS):
+            load_chunk(c)
+        pairs = ROW_TILES // PAIR
+        for pair in range(pairs):
+            sort(chunks[0], pair)
+        done = 0
+        for c, chunk in enumerate(chunks):
+            load_chunk(c + CHUNK_BUFFERS)
+            rounds = len(chunk["items"])
+            for s, item in enumerate(chunk["items"]):
+                transpose_pass(item)
+                done += 1
+                if done > QUANTISE_LAG:
+                    quantise_pass(items[done - 1 - QUANTISE_LAG])
+                if c + 1 < len(chunks):
+                    for pair in range(s * pairs // rounds, (s + 1) * pairs // rounds):
+                        sort(chunks[c + 1], pair)
+                if done > MULTIPLY_LAG:
+                    multiply(items[done - 1 - MULTIPLY_LAG])
+                if c == YBR_CHUNK and s == 0:
+                    prepare_small()
+                if c == YBR_CHUNK and s == QUANTISE_LAG:
+                    quantise_ybr()
+        for item in items[done - QUANTISE_LAG :]:
+            quantise_pass(item)
+        for item in items[done - MULTIPLY_LAG :]:
+            multiply(item)
 
-        d_grouped = [
-            keep.tile([P, P, IM_TILES], BF16, name="d_grouped%d" % bt, align_bytes=64)
-            for bt in range(VOLT_TILES)
-        ]
-        for t in range(IM_TILES):
-            for bt, copy in enumerate((nc.scalar.copy, nc.vector.tensor_copy)):
-                copy(out=d_grouped[bt][:, :, t], in_=d_sums[t][:, bt * P : (bt + 1) * P])
-
+        copies = [nc.scalar.copy, nc.vector.tensor_copy]
+        d_rows = []
+        for bt in range(VOLT_TILES):
+            rows = keep.tile([P, L2], BF16, name="d_rows%d" % bt, align_bytes=64)
+            copies[bt](out=rows[:], in_=d_sums[bt][:])
+            d_rows.append(rows)
+        d_grouped = []
+        for bt in range(VOLT_TILES):
+            words = d_rows[bt][:].bitcast(F32)
+            bank = banks.tile([P, 2, P], F32, tag="bank")
+            for u in range(2):
+                nc.tensor.transpose(bank[:, u, :], words[:, u : L2 // 2 : 2], ident[:])
+            grouped = keep.tile([P, L2], BF16, name="d_grouped%d" % bt, align_bytes=64)
+            copies[bt](
+                out=grouped[:].bitcast(F32).rearrange("p (c w u) -> p c u w", w=2, u=2),
+                in_=bank[:].rearrange("p u (c w) -> p c u w", w=2),
+            )
+            d_grouped.append(grouped)
         currents = []
         for bt in range(VOLT_TILES):
             d_codes = keep.tile([P, P], U32, name="d_codes%d" % bt, align_bytes=64)
             d_scales = keep.tile([P, P], U8, name="d_scales%d" % bt, align_bytes=64)
             nc.vector.quantize_mx(
-                out=d_codes[:].bitcast(FP8X4),
-                scales=d_scales[:],
-                in_=d_grouped[bt][:].rearrange("p b t -> p (b t)"),
+                out=d_codes[:].bitcast(FP8X4), scales=d_scales[:], in_=d_grouped[bt][:]
             )
             ibr = banks.tile([P, L2], F32, tag="bank")
             nc.tensor.matmul_mx(
@@ -264,46 +303,65 @@ def tile_kktloss_pa_k_kernel(tc, Volt, IM, Ybr, L_limit, n_o_mu_i_u, out):
 
         squares = []
         for bt in range(VOLT_TILES):
-            square = tail.tile([P, L2], F32)
-            nc.scalar.activation(out=square[:], in_=currents[bt][:], func=ACT.Square)
-            squares.append(square)
-
+            halves = []
+            for half in range(2):
+                square = tail.tile([P, NL], F32, name="square%d" % half)
+                nc.scalar.activation(
+                    out=square[:],
+                    in_=currents[bt][:, half * NL : (half + 1) * NL],
+                    func=ACT.Square,
+                )
+                halves.append(square)
+            squares.append(halves)
+        weighted = []
+        partial_sums = []
         for bt in range(VOLT_TILES):
-            magnitude = tail.tile([P, NL], F32)
+            real_excess = tail.tile([P, NL], F32)
             nc.vector.tensor_tensor(
-                out=magnitude[:], in0=squares[bt][:, :NL], in1=squares[bt][:, NL:], op=ALU.add
+                out=real_excess[:], in0=squares[bt][0][:], in1=limit_sq[:], op=ALU.subtract
             )
             excess = tail.tile([P, NL], F32)
-            nc.vector.tensor_tensor(
-                out=excess[:], in0=magnitude[:], in1=limit_sq[:], op=ALU.subtract
-            )
-            over = tail.tile([P, NL], F32)
-            over_sum = tail.tile([P, 1], F32)
-            nc.scalar.activation(
-                out=over[:], in_=excess[:], func=ACT.Relu, accum_out=over_sum[:]
-            )
-            slack = tail.tile([P, NL], F32)
-            nc.vector.tensor_tensor(
-                out=slack[:], in0=excess[:], in1=mu[:, bt * NL : (bt + 1) * NL], op=ALU.mult
-            )
-            slack_abs = tail.tile([P, NL], F32)
-            slack_sum = tail.tile([P, 1], F32)
+            excess_sum = tail.tile([P, 1], F32)
             nc.vector.scalar_tensor_tensor(
-                out=slack_abs[:],
-                in0=slack[:],
-                scalar=-1.0,
-                in1=slack[:],
+                out=excess[:],
+                in0=squares[bt][1][:],
+                scalar=1.0,
+                in1=real_excess[:],
                 op0=ALU.mult,
-                op1=ALU.max,
-                accum_out=slack_sum[:],
-            )
-            nc.vector.tensor_scalar(
-                out=result_cols[:, bt : bt + 1],
-                in0=slack_sum[:],
-                scalar1=over_sum[:],
-                scalar2=neg_mu_sums[bt][:],
-                op0=ALU.add,
                 op1=ALU.add,
+                accum_out=excess_sum[:],
+            )
+            product = tail.tile([P, NL], F32)
+            nc.vector.scalar_tensor_tensor(
+                out=product[:],
+                in0=mu_abs[:, bt * NL : (bt + 1) * NL],
+                scalar=0.5,
+                in1=excess[:],
+                op0=ALU.add,
+                op1=ALU.mult,
+            )
+            weighted.append(product)
+            partial_sum = tail.tile([P, 1], F32)
+            nc.vector.scalar_tensor_tensor(
+                out=partial_sum[:],
+                in0=excess_sum[:],
+                scalar=0.5,
+                in1=neg_mu_sums[bt][:],
+                op0=ALU.mult,
+                op1=ALU.add,
+            )
+            partial_sums.append(partial_sum)
+        for bt in range(VOLT_TILES):
+            magnitude = tail.tile([P, NL], F32)
+            magnitude_sum = tail.tile([P, 1], F32)
+            nc.scalar.activation(
+                out=magnitude[:], in_=weighted[bt][:], func=ACT.Abs, accum_out=magnitude_sum[:]
+            )
+            nc.vector.tensor_tensor(
+                out=result_cols[:, bt : bt + 1],
+                in0=magnitude_sum[:],
+                in1=partial_sums[bt][:],
+                op=ALU.add,
             )
 
         flipped = banks.tile([P, P], F32, tag="bank")

@@ -25,12 +25,10 @@ IM_TILES = L2 // P
 ROW_TILES = VOLT_TILES + IM_TILES
 PAIR = 2
 
-CHUNKS = [512, 512] + 3 * [1024] + 5 * [2048] + [1024, 512, 512]
-CHUNK_BUFFERS = 3
-VOLT_PASSES = 2
-YBR_CHUNK = 5
-QUANTISE_LAG = 2
-MULTIPLY_LAG = 4
+CHUNKS = 4 * [512] + 13 * [1024] + 2 * [512]
+FIRST_SORTED = 3
+CHUNK_BUFFERS = 6
+YBR_CHUNK = 10
 
 FLOPS = 2 * BATCH * L2 * N2 + 2 * BATCH * L2 * L2
 
@@ -41,8 +39,8 @@ def tile_kktloss_pa_k_kernel(tc, Volt, IM, Ybr, L_limit, n_o_mu_i_u, out):
         keep = ctx.enter_context(tc.tile_pool(name="keep", bufs=1))
         raw_in = ctx.enter_context(tc.tile_pool(name="raw_in", bufs=CHUNK_BUFFERS))
         sorted_in = ctx.enter_context(tc.tile_pool(name="sorted_in", bufs=2))
-        regroup = ctx.enter_context(tc.tile_pool(name="regroup", bufs=4))
-        mx = ctx.enter_context(tc.tile_pool(name="mx", bufs=6))
+        regroup = ctx.enter_context(tc.tile_pool(name="regroup", bufs=2))
+        mx = ctx.enter_context(tc.tile_pool(name="mx", bufs=3))
         tail = ctx.enter_context(tc.tile_pool(name="tail", bufs=2))
         sums = ctx.enter_context(tc.psum_pool(name="sums", bufs=1))
         banks = ctx.enter_context(tc.psum_pool(name="banks", bufs=6))
@@ -64,119 +62,102 @@ def tile_kktloss_pa_k_kernel(tc, Volt, IM, Ybr, L_limit, n_o_mu_i_u, out):
         volt_rows = Volt.rearrange("(t p) k -> p t k", p=P)
         im_rows = IM.rearrange("(t p) k -> p t k", p=P)
 
-        def transpose(halves, grouped, copies):
-            words = grouped.bitcast(F32).rearrange("p (b c w u) -> p b c u w", c=P, w=2, u=2)
-            for first in range(0, len(halves), 2):
-                bank = banks.tile([P, 2, 2 * P], F32, tag="bank")
-                for i in range(2):
-                    for u in range(2):
-                        nc.tensor.transpose(
-                            bank[:, u, i * P : (i + 1) * P], halves[first + i][u], ident[:]
-                        )
-                copies[first // 2 % len(copies)](
-                    out=words[:, first // 2],
-                    in_=bank[:].rearrange("p u (c w) -> p c u w", w=2),
-                )
+        def transpose_bank(halves, grouped):
+            bank = banks.tile([P, 2, 2 * P], F32, tag="bank")
+            for i in range(2):
+                for u in range(2):
+                    nc.tensor.transpose(bank[:, u, i * P : (i + 1) * P], halves[i][u], ident[:])
+            nc.scalar.copy(
+                out=grouped.bitcast(F32).rearrange("p (c w u) -> p c u w", w=2, u=2),
+                in_=bank[:].rearrange("p u (c w) -> p c u w", w=2),
+            )
 
         def load(chunk):
             width, cols = chunk["width"], chunk["cols"]
-            chunk["raw"] = []
-            for name, rows in (
-                ("volt_raw", volt_rows),
-                ("im_raw0", im_rows[:, :PAIR, :]),
-                ("im_raw1", im_rows[:, PAIR:, :]),
+            raw = raw_in.tile([P, ROW_TILES, width], BF16, align_bytes=64)
+            for first, rows in (
+                (0, volt_rows),
+                (VOLT_TILES, im_rows[:, :PAIR, :]),
+                (VOLT_TILES + PAIR, im_rows[:, PAIR:, :]),
             ):
-                raw = raw_in.tile([P, PAIR * width], BF16, name=name, align_bytes=64)
-                nc.sync.dma_start(
-                    out=raw[:].rearrange("p (t k) -> p t k", t=PAIR), in_=rows[:, :, cols]
-                )
-                chunk["raw"].append(raw)
+                nc.sync.dma_start(out=raw[:, first : first + PAIR, :], in_=rows[:, :, cols])
+            chunk["raw"] = raw
 
-        def sort(chunk, pair):
-            in_order = sorted_in.tile(
-                [P, PAIR * chunk["width"]], BF16, name="in_order%d" % pair, align_bytes=64
-            )
-            nc.vector.tensor_copy(
-                out=in_order[:].rearrange("p (u n x) -> p u n x", u=2, x=RUN),
-                in_=chunk["raw"][pair][:].rearrange("p (n u x) -> p u n x", u=2, x=RUN),
-            )
-            words = in_order[:].bitcast(F32).rearrange("p (u r w) -> p u r w", u=2, r=PAIR)
-            chunk["words"] += [words[:, :, r] for r in range(PAIR)]
+        def is_sorted(chunk, g):
+            index = chunk["cols"].start // K_PASS + g
+            return index >= FIRST_SORTED and index % 2 == 1
 
-        def blocks(chunk, g, tiles):
-            cols = slice(g * P, (g + 1) * P)
-            return [[chunk["words"][t][:, u, cols] for u in range(2)] for t in tiles]
+        def sort(chunk):
+            for g in range(chunk["passes"]):
+                if is_sorted(chunk, g):
+                    in_order = sorted_in.tile([P, 2, ROW_TILES, K_PASS // 2], BF16, align_bytes=64)
+                    runs = chunk["raw"][:, :, g * K_PASS : (g + 1) * K_PASS].rearrange(
+                        "p r (n u x) -> p u r n x", u=2, x=RUN
+                    )
+                    for u in range(2):
+                        nc.vector.tensor_copy(
+                            out=in_order[:, u].rearrange("p r (n x) -> p r n x", x=RUN),
+                            in_=runs[:, u],
+                        )
+                    chunk["sorted"] = in_order
 
-        def quantise(operand):
-            columns = operand["columns"]
-            codes = mx.tile([P, columns], U32, name=operand["name"] + "_codes", align_bytes=64)
-            scales = mx.tile([P, columns], U8, name=operand["name"] + "_scales", align_bytes=64)
-            nc.vector.quantize_mx(
-                out=codes[:].bitcast(FP8X4), scales=scales[:], in_=operand["grouped"][:]
-            )
-            operand["mx"] = (codes, scales)
+        def halves(chunk, g, r):
+            if is_sorted(chunk, g):
+                return [chunk["sorted"][:, u, r, :].bitcast(F32) for u in range(2)]
+            words = chunk["raw"][:, r, g * K_PASS : (g + 1) * K_PASS].bitcast(F32)
+            return [words[:, u : K_PASS // 2 : 2] for u in range(2)]
 
-        def transpose_pass(item):
-            chunk, g = item["chunk"], item["pass"]
-            volt = item["volt"]
-            if "grouped" not in volt:
-                volt["grouped"] = regroup.tile(
-                    [P, 4 * volt["columns"]], BF16, name="volt_grouped", align_bytes=64
-                )
-            first = item["volt_column"] * 4
-            transpose(
-                blocks(chunk, g, range(VOLT_TILES)),
-                volt["grouped"][:, first : first + 4 * BATCH],
-                [nc.scalar.copy],
-            )
-            grouped = regroup.tile([P, 4 * L2], BF16, name="im_grouped", align_bytes=64)
-            transpose(
-                blocks(chunk, g, range(VOLT_TILES, ROW_TILES)), grouped[:], [nc.scalar.copy]
-            )
-            item["im"] = {"name": "im", "columns": L2, "grouped": grouped}
+        def transpose(chunk):
+            passes = chunk["passes"]
+            volt = regroup.tile([P, passes * 4 * BATCH], BF16, name="volt_grouped", align_bytes=64)
+            im = [
+                regroup.tile([P, 4 * L2], BF16, name="im_grouped%d" % g, align_bytes=64)
+                for g in range(passes)
+            ]
+            for first in range(0, ROW_TILES, PAIR):
+                for g in range(passes):
+                    if first < VOLT_TILES:
+                        grouped = volt[:, g * 4 * BATCH : (g + 1) * 4 * BATCH]
+                    else:
+                        column = (first - VOLT_TILES) * K_PASS
+                        grouped = im[g][:, column : column + PAIR * K_PASS]
+                    transpose_bank([halves(chunk, g, first + i) for i in range(PAIR)], grouped)
+            chunk["grouped"] = [volt] + im
 
-        def quantise_pass(item):
-            if item["closes_volt"]:
-                quantise(item["volt"])
-            quantise(item["im"])
+        def quantise_tile(grouped, codes, scales):
+            nc.vector.quantize_mx(out=codes[:].bitcast(FP8X4), scales=scales[:], in_=grouped[:])
 
-        def multiply(item):
-            (volt_codes, volt_scales), (im_codes, im_scales) = item["volt"]["mx"], item["im"]["mx"]
+        def quantise(chunk):
+            chunk["mx"] = []
+            for i, grouped in enumerate(chunk["grouped"]):
+                columns = chunk["passes"] * BATCH if i == 0 else L2
+                codes = mx.tile([P, columns], U32, name="codes%d" % i, align_bytes=64)
+                scales = mx.tile([P, columns], U8, name="scales%d" % i, align_bytes=64)
+                quantise_tile(grouped, codes, scales)
+                chunk["mx"].append((codes, scales))
+
+        def multiply(chunk):
+            volt_codes, volt_scales = chunk["mx"][0]
             for bt in range(VOLT_TILES):
-                first = item["volt_column"] + bt * P
-                nc.tensor.matmul_mx(
-                    out=d_sums[bt][:],
-                    lhsT=volt_codes[:, first : first + P].bitcast(FP8X4),
-                    lhsT_scale=volt_scales[:, first : first + P],
-                    rhs=im_codes[:].bitcast(FP8X4),
-                    rhs_scale=im_scales[:],
-                    start=item["first"],
-                    stop=item["last"],
-                )
+                for g in range(chunk["passes"]):
+                    im_codes, im_scales = chunk["mx"][1 + g]
+                    rows = slice(g * BATCH + bt * P, g * BATCH + (bt + 1) * P)
+                    nc.tensor.matmul_mx(
+                        out=d_sums[bt][:],
+                        lhsT=volt_codes[:, rows].bitcast(FP8X4),
+                        lhsT_scale=volt_scales[:, rows],
+                        rhs=im_codes[:].bitcast(FP8X4),
+                        rhs_scale=im_scales[:],
+                        start=(chunk["cols"].start == 0 and g == 0),
+                        stop=(chunk["cols"].stop == N2 and g == chunk["passes"] - 1),
+                    )
 
         chunks = []
-        items = []
         start_col = 0
         for width in CHUNKS:
-            chunk = {"width": width, "cols": slice(start_col, start_col + width), "words": []}
+            cols = slice(start_col, start_col + width)
+            chunks.append({"width": width, "cols": cols, "passes": width // K_PASS})
             start_col += width
-            chunk["items"] = []
-            for g in range(width // K_PASS):
-                if g % VOLT_PASSES == 0:
-                    together = min(VOLT_PASSES, width // K_PASS - g)
-                    volt = {"name": "volt", "columns": together * BATCH}
-                item = {
-                    "chunk": chunk,
-                    "pass": g,
-                    "volt": volt,
-                    "volt_column": g % VOLT_PASSES * BATCH,
-                    "closes_volt": g % VOLT_PASSES == together - 1,
-                    "first": len(items) == 0,
-                    "last": len(items) == N2 // K_PASS - 1,
-                }
-                chunk["items"].append(item)
-                items.append(item)
-            chunks.append(chunk)
 
         ybr_raw = keep.tile([P, IM_TILES * L2], BF16)
         mu = keep.tile([P, VOLT_TILES * NL], BF16)
@@ -205,11 +186,14 @@ def tile_kktloss_pa_k_kernel(tc, Volt, IM, Ybr, L_limit, n_o_mu_i_u, out):
 
         def prepare_small():
             words = ybr_raw[:].bitcast(F32).rearrange("p (t w) -> p t w", t=IM_TILES)
-            transpose(
-                [[words[:, t, u : L2 // 2 : 2] for u in range(2)] for t in range(IM_TILES)],
-                ybr_grouped[:],
-                [nc.scalar.copy],
-            )
+            for first in range(0, IM_TILES, PAIR):
+                transpose_bank(
+                    [
+                        [words[:, first + i, u : L2 // 2 : 2] for u in range(2)]
+                        for i in range(PAIR)
+                    ],
+                    ybr_grouped[:, first * L2 : (first + PAIR) * L2],
+                )
             limit_all = banks.tile([P, NL], F32, tag="bank")
             nc.tensor.matmul(
                 out=limit_all[:], lhsT=ones[:], rhs=limit_row[:], start=True, stop=True
@@ -225,50 +209,35 @@ def tile_kktloss_pa_k_kernel(tc, Volt, IM, Ybr, L_limit, n_o_mu_i_u, out):
                     accum_out=neg_mu_sums[bt][:],
                 )
 
-        def quantise_ybr():
-            nc.vector.quantize_mx(
-                out=ybr_codes[:].bitcast(FP8X4), scales=ybr_scales[:], in_=ybr_grouped[:]
-            )
-
         def load_chunk(c):
+            if c == YBR_CHUNK:
+                load_small()
             if c < len(chunks):
                 load(chunks[c])
-            if c == YBR_CHUNK - 1:
-                load_small()
 
         for c in range(CHUNK_BUFFERS):
             load_chunk(c)
-        pairs = ROW_TILES // PAIR
-        for pair in range(pairs):
-            sort(chunks[0], pair)
-        done = 0
-        for c, chunk in enumerate(chunks):
-            load_chunk(c + CHUNK_BUFFERS)
-            rounds = len(chunk["items"])
-            for s, item in enumerate(chunk["items"]):
-                transpose_pass(item)
-                done += 1
-                if done > QUANTISE_LAG:
-                    quantise_pass(items[done - 1 - QUANTISE_LAG])
-                if c + 1 < len(chunks):
-                    for pair in range(s * pairs // rounds, (s + 1) * pairs // rounds):
-                        sort(chunks[c + 1], pair)
-                if done > MULTIPLY_LAG:
-                    multiply(items[done - 1 - MULTIPLY_LAG])
-                if c == YBR_CHUNK and s == 0:
-                    prepare_small()
-                if c == YBR_CHUNK and s == QUANTISE_LAG:
-                    quantise_ybr()
-        for item in items[done - QUANTISE_LAG :]:
-            quantise_pass(item)
-        for item in items[done - MULTIPLY_LAG :]:
-            multiply(item)
+        sort(chunks[0])
+        for c in range(len(chunks) + 2):
+            if 0 <= c - 1 < len(chunks):
+                quantise(chunks[c - 1])
+            if c == YBR_CHUNK + 1:
+                quantise_tile(ybr_grouped, ybr_codes, ybr_scales)
+            if c + 1 < len(chunks):
+                sort(chunks[c + 1])
+            if c < len(chunks):
+                transpose(chunks[c])
+                load_chunk(c + CHUNK_BUFFERS)
+            if c == YBR_CHUNK:
+                prepare_small()
+            if 0 <= c - 2:
+                multiply(chunks[c - 2])
 
-        copies = [nc.scalar.copy, nc.vector.tensor_copy]
         d_rows = []
         for bt in range(VOLT_TILES):
             rows = keep.tile([P, L2], BF16, name="d_rows%d" % bt, align_bytes=64)
-            copies[bt](out=rows[:], in_=d_sums[bt][:])
+            nc.scalar.copy(out=rows[:, :NL], in_=d_sums[bt][:, :NL])
+            nc.vector.tensor_copy(out=rows[:, NL:], in_=d_sums[bt][:, NL:])
             d_rows.append(rows)
         d_grouped = []
         for bt in range(VOLT_TILES):
@@ -277,7 +246,7 @@ def tile_kktloss_pa_k_kernel(tc, Volt, IM, Ybr, L_limit, n_o_mu_i_u, out):
             for u in range(2):
                 nc.tensor.transpose(bank[:, u, :], words[:, u : L2 // 2 : 2], ident[:])
             grouped = keep.tile([P, L2], BF16, name="d_grouped%d" % bt, align_bytes=64)
-            copies[bt](
+            nc.scalar.copy(
                 out=grouped[:].bitcast(F32).rearrange("p (c w u) -> p c u w", w=2, u=2),
                 in_=bank[:].rearrange("p u (c w) -> p c u w", w=2),
             )
@@ -354,9 +323,23 @@ def tile_kktloss_pa_k_kernel(tc, Volt, IM, Ybr, L_limit, n_o_mu_i_u, out):
         for bt in range(VOLT_TILES):
             magnitude = tail.tile([P, NL], F32)
             magnitude_sum = tail.tile([P, 1], F32)
-            nc.scalar.activation(
-                out=magnitude[:], in_=weighted[bt][:], func=ACT.Abs, accum_out=magnitude_sum[:]
-            )
+            if bt == 0:
+                nc.scalar.activation(
+                    out=magnitude[:],
+                    in_=weighted[bt][:],
+                    func=ACT.Abs,
+                    accum_out=magnitude_sum[:],
+                )
+            else:
+                nc.vector.scalar_tensor_tensor(
+                    out=magnitude[:],
+                    in0=weighted[bt][:],
+                    scalar=-1.0,
+                    in1=weighted[bt][:],
+                    op0=ALU.mult,
+                    op1=ALU.max,
+                    accum_out=magnitude_sum[:],
+                )
             nc.vector.tensor_tensor(
                 out=result_cols[:, bt : bt + 1],
                 in0=magnitude_sum[:],

@@ -62,12 +62,12 @@ def tile_kktloss_pa_k_kernel(tc, Volt, IM, Ybr, L_limit, n_o_mu_i_u, out):
         volt_rows = Volt.rearrange("(t p) k -> p t k", p=P)
         im_rows = IM.rearrange("(t p) k -> p t k", p=P)
 
-        def transpose_bank(halves, grouped):
+        def transpose_bank(halves, grouped, copy):
             bank = banks.tile([P, 2, 2 * P], F32, tag="bank")
             for i in range(2):
                 for u in range(2):
                     nc.tensor.transpose(bank[:, u, i * P : (i + 1) * P], halves[i][u], ident[:])
-            nc.scalar.copy(
+            copy(
                 out=grouped.bitcast(F32).rearrange("p (c w u) -> p c u w", w=2, u=2),
                 in_=bank[:].rearrange("p u (c w) -> p c u w", w=2),
             )
@@ -121,7 +121,12 @@ def tile_kktloss_pa_k_kernel(tc, Volt, IM, Ybr, L_limit, n_o_mu_i_u, out):
                     else:
                         column = (first - VOLT_TILES) * K_PASS
                         grouped = im[g][:, column : column + PAIR * K_PASS]
-                    transpose_bank([halves(chunk, g, first + i) for i in range(PAIR)], grouped)
+                    last = passes > 1 and g == passes - 1 and first == ROW_TILES - PAIR
+                    transpose_bank(
+                        [halves(chunk, g, first + i) for i in range(PAIR)],
+                        grouped,
+                        nc.vector.tensor_copy if last else nc.scalar.copy,
+                    )
             chunk["grouped"] = [volt] + im
 
         def quantise_tile(grouped, codes, scales):
@@ -193,6 +198,7 @@ def tile_kktloss_pa_k_kernel(tc, Volt, IM, Ybr, L_limit, n_o_mu_i_u, out):
                         for i in range(PAIR)
                     ],
                     ybr_grouped[:, first * L2 : (first + PAIR) * L2],
+                    nc.scalar.copy,
                 )
             limit_all = banks.tile([P, NL], F32, tag="bank")
             nc.tensor.matmul(

from contextlib import ExitStack

import concourse.mybir as mybir
from concourse.masks import make_identity

F32 = mybir.dt.float32
BF16 = mybir.dt.bfloat16
U32 = mybir.dt.uint32
U8 = mybir.dt.uint8
FP8X4 = mybir.dt.float8_e4m3fn_x4
ALU = mybir.AluOpType
ACT = mybir.ActivationFunctionType

P = 128
K_PASS = 512
RUN = 16

BATCH = 256
N2 = 16384
L2 = 512
NL = L2 // 2

VOLT_TILES = BATCH // P
IM_TILES = L2 // P
ROW_TILES = VOLT_TILES + IM_TILES
PAIR = 2

CHUNKS = 4 * [512] + 13 * [1024] + 2 * [512]
FIRST_SORTED = 3
CHUNK_BUFFERS = 6
YBR_CHUNK = 10

FLOPS = 2 * BATCH * L2 * N2 + 2 * BATCH * L2 * L2


def tile_kktloss_pa_k_kernel(tc, Volt, IM, Ybr, L_limit, n_o_mu_i_u, out):
    nc = tc.nc
    with ExitStack() as ctx:
        keep = ctx.enter_context(tc.tile_pool(name="keep", bufs=1))
        raw_in = ctx.enter_context(tc.tile_pool(name="raw_in", bufs=CHUNK_BUFFERS))
        sorted_in = ctx.enter_context(tc.tile_pool(name="sorted_in", bufs=2))
        regroup = ctx.enter_context(tc.tile_pool(name="regroup", bufs=2))
        mx = ctx.enter_context(tc.tile_pool(name="mx", bufs=3))
        tail = ctx.enter_context(tc.tile_pool(name="tail", bufs=2))
        sums = ctx.enter_context(tc.psum_pool(name="sums", bufs=1))
        banks = ctx.enter_context(tc.psum_pool(name="banks", bufs=6))
        ctx.enter_context(tc.manual_schedule())

        ident = keep.tile([P, P], F32)
        make_identity(nc, ident[:])
        ones = keep.tile([P, P], BF16)
        nc.vector.memset(ones[:], 1.0)
        result_cols = keep.tile([P, P], F32)
        nc.vector.memset(result_cols[:], 0.0)
        limit_row = keep.tile([P, NL], BF16)
        nc.vector.memset(limit_row[:], 0.0)

        d_sums = [
            sums.tile([P, L2], F32, name="d_sum%d" % bt) for bt in range(VOLT_TILES)
        ]

        volt_rows = Volt.rearrange("(t p) k -> p t k", p=P)
        im_rows = IM.rearrange("(t p) k -> p t k", p=P)

        def transpose_bank(halves, grouped, copy):
            bank = banks.tile([P, 2, 2 * P], F32, tag="bank")
            for i in range(2):
                for u in range(2):
                    nc.tensor.transpose(bank[:, u, i * P : (i + 1) * P], halves[i][u], ident[:])
            copy(
                out=grouped.bitcast(F32).rearrange("p (c w u) -> p c u w", w=2, u=2),
                in_=bank[:].rearrange("p u (c w) -> p c u w", w=2),
            )

        def load(chunk):
            width, cols = chunk["width"], chunk["cols"]
            raw = raw_in.tile([P, ROW_TILES, width], BF16, align_bytes=64)
            for first, rows in (
                (0, volt_rows),
                (VOLT_TILES, im_rows[:, :PAIR, :]),
                (VOLT_TILES + PAIR, im_rows[:, PAIR:, :]),
            ):
                nc.sync.dma_start(out=raw[:, first : first + PAIR, :], in_=rows[:, :, cols])
            chunk["raw"] = raw

        def is_sorted(chunk, g):
            index = chunk["cols"].start // K_PASS + g
            return index >= FIRST_SORTED and index % 2 == 1

        def sort(chunk):
            for g in range(chunk["passes"]):
                if is_sorted(chunk, g):
                    in_order = sorted_in.tile([P, 2, ROW_TILES, K_PASS // 2], BF16, align_bytes=64)
                    runs = chunk["raw"][:, :, g * K_PASS : (g + 1) * K_PASS].rearrange(
                        "p r (n u x) -> p u r n x", u=2, x=RUN
                    )
                    for u in range(2):
                        nc.vector.tensor_copy(
                            out=in_order[:, u].rearrange("p r (n x) -> p r n x", x=RUN),
                            in_=runs[:, u],
                        )
                    chunk["sorted"] = in_order

        def halves(chunk, g, r):
            if is_sorted(chunk, g):
                return [chunk["sorted"][:, u, r, :].bitcast(F32) for u in range(2)]
            words = chunk["raw"][:, r, g * K_PASS : (g + 1) * K_PASS].bitcast(F32)
            return [words[:, u : K_PASS // 2 : 2] for u in range(2)]

        def transpose(chunk):
            passes = chunk["passes"]
            volt = regroup.tile([P, passes * 4 * BATCH], BF16, name="volt_grouped", align_bytes=64)
            im = [
                regroup.tile([P, 4 * L2], BF16, name="im_grouped%d" % g, align_bytes=64)
                for g in range(passes)
            ]
            for first in range(0, ROW_TILES, PAIR):
                for g in range(passes):
                    if first < VOLT_TILES:
                        grouped = volt[:, g * 4 * BATCH : (g + 1) * 4 * BATCH]
                    else:
                        column = (first - VOLT_TILES) * K_PASS
                        grouped = im[g][:, column : column + PAIR * K_PASS]
                    last = passes > 1 and g == passes - 1 and first == ROW_TILES - PAIR
                    transpose_bank(
                        [halves(chunk, g, first + i) for i in range(PAIR)],
                        grouped,
                        nc.vector.tensor_copy if last else nc.scalar.copy,
                    )
            chunk["grouped"] = [volt] + im

        def quantise_tile(grouped, codes, scales):
            nc.vector.quantize_mx(out=codes[:].bitcast(FP8X4), scales=scales[:], in_=grouped[:])

        def quantise(chunk):
            chunk["mx"] = []
            for i, grouped in enumerate(chunk["grouped"]):
                columns = chunk["passes"] * BATCH if i == 0 else L2
                codes = mx.tile([P, columns], U32, name="codes%d" % i, align_bytes=64)
                scales = mx.tile([P, columns], U8, name="scales%d" % i, align_bytes=64)
                quantise_tile(grouped, codes, scales)
                chunk["mx"].append((codes, scales))

        def multiply(chunk):
            volt_codes, volt_scales = chunk["mx"][0]
            for bt in range(VOLT_TILES):
                for g in range(chunk["passes"]):
                    im_codes, im_scales = chunk["mx"][1 + g]
                    rows = slice(g * BATCH + bt * P, g * BATCH + (bt + 1) * P)
                    nc.tensor.matmul_mx(
                        out=d_sums[bt][:],
                        lhsT=volt_codes[:, rows].bitcast(FP8X4),
                        lhsT_scale=volt_scales[:, rows],
                        rhs=im_codes[:].bitcast(FP8X4),
                        rhs_scale=im_scales[:],
                        start=(chunk["cols"].start == 0 and g == 0),
                        stop=(chunk["cols"].stop == N2 and g == chunk["passes"] - 1),
                    )

        chunks = []
        start_col = 0
        for width in CHUNKS:
            cols = slice(start_col, start_col + width)
            chunks.append({"width": width, "cols": cols, "passes": width // K_PASS})
            start_col += width

        ybr_raw = keep.tile([P, IM_TILES * L2], BF16)
        mu = keep.tile([P, VOLT_TILES * NL], BF16)
        ybr_grouped = keep.tile([P, IM_TILES * L2], BF16, align_bytes=64)
        ybr_codes = keep.tile([P, L2], U32, align_bytes=64)
        ybr_scales = keep.tile([P, L2], U8, align_bytes=64)
        limit_sq = keep.tile([P, NL], F32)
        mu_abs = keep.tile([P, VOLT_TILES * NL], F32)
        neg_mu = keep.tile([P, NL], F32)
        neg_mu_sums = [
            keep.tile([P, 1], F32, name="neg_mu_sum%d" % bt) for bt in range(VOLT_TILES)
        ]

        def load_small():
            nc.sync.dma_start(
                out=ybr_raw[:].rearrange("p (t j) -> p t j", t=IM_TILES),
                in_=Ybr.rearrange("(t p) j -> p t j", p=P),
            )
            nc.sync.dma_start(
                out=mu[:].rearrange("p (t l) -> p t l", t=VOLT_TILES),
                in_=n_o_mu_i_u.rearrange("(t p) l -> p t l", p=P),
            )
            nc.sync.dma_start(
                out=limit_row[0:1, :], in_=L_limit.rearrange("(o l) -> o l", o=1)
            )

        def prepare_small():
            words = ybr_raw[:].bitcast(F32).rearrange("p (t w) -> p t w", t=IM_TILES)
            for first in range(0, IM_TILES, PAIR):
                transpose_bank(
                    [
                        [words[:, first + i, u : L2 // 2 : 2] for u in range(2)]
                        for i in range(PAIR)
                    ],
                    ybr_grouped[:, first * L2 : (first + PAIR) * L2],
                    nc.scalar.copy,
                )
            limit_all = banks.tile([P, NL], F32, tag="bank")
            nc.tensor.matmul(
                out=limit_all[:], lhsT=ones[:], rhs=limit_row[:], start=True, stop=True
            )
            nc.scalar.activation(out=limit_sq[:], in_=limit_all[:], func=ACT.Square)
            nc.scalar.activation(out=mu_abs[:], in_=mu[:], func=ACT.Abs)
            for bt in range(VOLT_TILES):
                nc.scalar.activation(
                    out=neg_mu[:],
                    in_=mu[:, bt * NL : (bt + 1) * NL],
                    func=ACT.Relu,
                    scale=-1.0,
                    accum_out=neg_mu_sums[bt][:],
                )

        def load_chunk(c):
            if c == YBR_CHUNK:
                load_small()
            if c < len(chunks):
                load(chunks[c])

        for c in range(CHUNK_BUFFERS):
            load_chunk(c)
        sort(chunks[0])
        for c in range(len(chunks) + 2):
            if 0 <= c - 1 < len(chunks):
                quantise(chunks[c - 1])
            if c == YBR_CHUNK + 1:
                quantise_tile(ybr_grouped, ybr_codes, ybr_scales)
            if c + 1 < len(chunks):
                sort(chunks[c + 1])
            if c < len(chunks):
                transpose(chunks[c])
                load_chunk(c + CHUNK_BUFFERS)
            if c == YBR_CHUNK:
                prepare_small()
            if 0 <= c - 2:
                multiply(chunks[c - 2])

        d_rows = []
        for bt in range(VOLT_TILES):
            rows = keep.tile([P, L2], BF16, name="d_rows%d" % bt, align_bytes=64)
            nc.scalar.copy(out=rows[:, :NL], in_=d_sums[bt][:, :NL])
            nc.vector.tensor_copy(out=rows[:, NL:], in_=d_sums[bt][:, NL:])
            d_rows.append(rows)
        d_grouped = []
        for bt in range(VOLT_TILES):
            words = d_rows[bt][:].bitcast(F32)
            bank = banks.tile([P, 2, P], F32, tag="bank")
            for u in range(2):
                nc.tensor.transpose(bank[:, u, :], words[:, u : L2 // 2 : 2], ident[:])
            grouped = keep.tile([P, L2], BF16, name="d_grouped%d" % bt, align_bytes=64)
            nc.scalar.copy(
                out=grouped[:].bitcast(F32).rearrange("p (c w u) -> p c u w", w=2, u=2),
                in_=bank[:].rearrange("p u (c w) -> p c u w", w=2),
            )
            d_grouped.append(grouped)
        currents = []
        for bt in range(VOLT_TILES):
            d_codes = keep.tile([P, P], U32, name="d_codes%d" % bt, align_bytes=64)
            d_scales = keep.tile([P, P], U8, name="d_scales%d" % bt, align_bytes=64)
            nc.vector.quantize_mx(
                out=d_codes[:].bitcast(FP8X4), scales=d_scales[:], in_=d_grouped[bt][:]
            )
            ibr = banks.tile([P, L2], F32, tag="bank")
            nc.tensor.matmul_mx(
                out=ibr[:],
                lhsT=d_codes[:].bitcast(FP8X4),
                lhsT_scale=d_scales[:],
                rhs=ybr_codes[:].bitcast(FP8X4),
                rhs_scale=ybr_scales[:],
                start=True,
                stop=True,
            )
            currents.append(ibr)

        squares = []
        for bt in range(VOLT_TILES):
            halves = []
            for half in range(2):
                square = tail.tile([P, NL], F32, name="square%d" % half)
                nc.scalar.activation(
                    out=square[:],
                    in_=currents[bt][:, half * NL : (half + 1) * NL],
                    func=ACT.Square,
                )
                halves.append(square)
            squares.append(halves)
        weighted = []
        partial_sums = []
        for bt in range(VOLT_TILES):
            real_excess = tail.tile([P, NL], F32)
            nc.vector.tensor_tensor(
                out=real_excess[:], in0=squares[bt][0][:], in1=limit_sq[:], op=ALU.subtract
            )
            excess = tail.tile([P, NL], F32)
            excess_sum = tail.tile([P, 1], F32)
            nc.vector.scalar_tensor_tensor(
                out=excess[:],
                in0=squares[bt][1][:],
                scalar=1.0,
                in1=real_excess[:],
                op0=ALU.mult,
                op1=ALU.add,
                accum_out=excess_sum[:],
            )
            product = tail.tile([P, NL], F32)
            nc.vector.scalar_tensor_tensor(
                out=product[:],
                in0=mu_abs[:, bt * NL : (bt + 1) * NL],
                scalar=0.5,
                in1=excess[:],
                op0=ALU.add,
                op1=ALU.mult,
            )
            weighted.append(product)
            partial_sum = tail.tile([P, 1], F32)
            nc.vector.scalar_tensor_tensor(
                out=partial_sum[:],
                in0=excess_sum[:],
                scalar=0.5,
                in1=neg_mu_sums[bt][:],
                op0=ALU.mult,
                op1=ALU.add,
            )
            partial_sums.append(partial_sum)
        for bt in range(VOLT_TILES):
            magnitude = tail.tile([P, NL], F32)
            magnitude_sum = tail.tile([P, 1], F32)
            if bt == 0:
                nc.scalar.activation(
                    out=magnitude[:],
                    in_=weighted[bt][:],
                    func=ACT.Abs,
                    accum_out=magnitude_sum[:],
                )
            else:
                nc.vector.scalar_tensor_tensor(
                    out=magnitude[:],
                    in0=weighted[bt][:],
                    scalar=-1.0,
                    in1=weighted[bt][:],
                    op0=ALU.mult,
                    op1=ALU.max,
                    accum_out=magnitude_sum[:],
                )
            nc.vector.tensor_tensor(
                out=result_cols[:, bt : bt + 1],
                in0=magnitude_sum[:],
                in1=partial_sums[bt][:],
                op=ALU.add,
            )

        flipped = banks.tile([P, P], F32, tag="bank")
        nc.tensor.transpose(flipped[:], result_cols[:], ident[:])
        result_rows = keep.tile([P, P], F32)
        nc.vector.tensor_copy(out=result_rows[:], in_=flipped[:])
        nc.sync.dma_start(
            out=out.rearrange("(t b) -> t b", t=VOLT_TILES),
            in_=result_rows[0:VOLT_TILES, :],
        )
